import numpy as np
import ml_dtypes

BF16 = ml_dtypes.bfloat16


def bf(x):
    return np.asarray(x, np.float32).astype(BF16)


def f32(x):
    return np.asarray(x, np.float32)


def f64(x):
    return np.asarray(x).astype(np.float64)


def striped(idx):
    return np.tile(idx.reshape(-1, 16).T, (8, 1))


V, E, H, N, NG = 2048, 128, 128, 512, 3


def sigmoid(a):
    return 1.0 / (1.0 + np.exp(-a))


def setup_inputs():
    return {
        "table": bf(np.random.standard_normal((E, V))),
        "context": bf(np.random.standard_normal((H, N))),
        "hid": bf(np.random.standard_normal((H, N))),
        "w_e": bf(np.random.standard_normal((E, NG * H)) / np.sqrt(E + H)),
        "w_c": bf(np.random.standard_normal((H, NG * H)) / np.sqrt(E + H)),
        "w_h": bf(np.random.standard_normal((H, NG * H)) / np.sqrt(H)),
        "b_ih": f32(0.3 * np.random.standard_normal((NG * H, 1))),
        "b_hh": f32(0.3 * np.random.standard_normal((NG * H, 1))),
        "offs": striped(np.random.permutation(np.tile(np.arange(V), 2))[:N]),
    }


def reference(table, context, hid, w_e, w_c, w_h, b_ih, b_hh, offs):
    idx = offs[:16].T.reshape(-1)
    h = f64(hid)
    a = (f64(w_e).T @ f64(table)[:, idx] + f64(w_c).T @ f64(context) + f64(b_ih)).reshape(NG, H, N)
    u = (f64(w_h).T @ h + f64(b_hh)).reshape(NG, H, N)
    r = sigmoid(a[0] + u[0])
    z = sigmoid(a[1] + u[1])
    n = np.tanh(a[2] + r * u[2])
    return (1.0 - z) * n + z * h

@@ -1,0 +1,79 @@
+import concourse.mybir as mybir
+
+P = 128
+V = 2048
+N = 512
+GATES = 3
+
+FLOPS = 2 * P * P * N * 9
+BYTES = (2 * (3 * P * N + 3 * P * GATES * P)
+         + 4 * 2 * GATES * P + 2 * N + 4 * P * N)
+
+BF16, F32, U16 = mybir.dt.bfloat16, mybir.dt.float32, mybir.dt.uint16
+ADD, SUB, MULT = mybir.AluOpType.add, mybir.AluOpType.subtract, mybir.AluOpType.mult
+SIGMOID, TANH = mybir.ActivationFunctionType.Sigmoid, mybir.ActivationFunctionType.Tanh
+
+
+def tile_attndecoderrnn_kernel(tc, table, context, hid, w_e, w_c, w_h, b_ih, b_hh, offs, out):
+    nc = tc.nc
+    with (
+        tc.tile_pool(name="held", bufs=1) as held,
+        tc.psum_pool(name="psum", bufs=1) as psum,
+    ):
+        offsets = held.tile([P, N // 16], U16, name="offsets")
+        nc.sync.dma_start(offsets[:], offs)
+        words = held.tile([P, V], BF16, name="words")
+        nc.sync.dma_start(words[:], table)
+        we = held.tile([P, GATES * P], BF16, name="we")
+        nc.scalar.dma_start(we[:], w_e)
+        wc = held.tile([P, GATES * P], BF16, name="wc")
+        nc.scalar.dma_start(wc[:], w_c)
+        ctx = held.tile([P, N], BF16, name="ctx")
+        nc.scalar.dma_start(ctx[:], context)
+        wh = held.tile([P, GATES * P], BF16, name="wh")
+        nc.gpsimd.dma_start(wh[:], w_h)
+        old = held.tile([P, N], BF16, name="old")
+        nc.gpsimd.dma_start(old[:], hid)
+        bih = held.tile([P, GATES], F32, name="bih")
+        bhh = held.tile([P, GATES], F32, name="bhh")
+        with nc.allow_non_contiguous_dma(reason="a bias of 384 floats, one to a partition"):
+            nc.gpsimd.dma_start(bih[:], b_ih.rearrange("(q m) o -> m (q o)", q=GATES))
+            nc.gpsimd.dma_start(bhh[:], b_hh.rearrange("(q m) o -> m (q o)", q=GATES))
+        bsum = held.tile([P, 2], F32, name="bsum")
+        nc.vector.tensor_tensor(bsum[:], bih[:, 0:2], bhh[:, 0:2], ADD)
+
+        def gate(w, q):
+            return w[:, q * P : (q + 1) * P]
+
+        picked = words[:].indirect(offsets[:])
+        acc_r = psum.tile([P, N], F32, name="acc_r")
+        acc_z = psum.tile([P, N], F32, name="acc_z")
+        acc_a = psum.tile([P, N], F32, name="acc_a")
+        acc_u = psum.tile([P, N], F32, name="acc_u")
+        nc.tensor.matmul(acc_r[:], gate(we, 0), picked, start=True, stop=False)
+        nc.tensor.matmul(acc_a[:], gate(we, 2), picked, start=True, stop=False)
+        nc.tensor.matmul(acc_z[:], gate(we, 1), picked, start=True, stop=False)
+        nc.tensor.matmul(acc_r[:], gate(wc, 0), ctx[:], start=False, stop=False)
+        nc.tensor.matmul(acc_r[:], gate(wh, 0), old[:], start=False, stop=True)
+        nc.tensor.matmul(acc_u[:], gate(wh, 2), old[:], start=True, stop=True)
+        nc.tensor.matmul(acc_a[:], gate(wc, 2), ctx[:], start=False, stop=True)
+        nc.tensor.matmul(acc_z[:], gate(wc, 1), ctx[:], start=False, stop=False)
+        nc.tensor.matmul(acc_z[:], gate(wh, 1), old[:], start=False, stop=True)
+
+        r = held.tile([P, N], F32, name="r")
+        nc.scalar.activation(r[:], acc_r[:], SIGMOID, bias=bsum[:, 0:1])
+        ru = held.tile([P, N], F32, name="ru")
+        nc.vector.scalar_tensor_tensor(ru[:], acc_u[:], bhh[:, 2:3], r[:], ADD, MULT)
+        pre = held.tile([P, N], F32, name="pre")
+        nc.vector.tensor_tensor(pre[:], ru[:], acc_a[:], ADD)
+        n = held.tile([P, N], F32, name="n")
+        nc.scalar.activation(n[:], pre[:], TANH, bias=bih[:, 2:3])
+        z = held.tile([P, N], F32, name="z")
+        nc.scalar.activation(z[:], acc_z[:], SIGMOID, bias=bsum[:, 1:2])
+        diff = held.tile([P, N], F32, name="diff")
+        nc.vector.tensor_tensor(diff[:], old[:], n[:], SUB)
+        step = held.tile([P, N], F32, name="step")
+        nc.vector.tensor_tensor(step[:], z[:], diff[:], MULT)
+        new = held.tile([P, N], F32, name="new")
+        nc.vector.tensor_tensor(new[:], n[:], step[:], ADD)
+        nc.sync.dma_start(out, new[:])

@@ -22,23 +22,23 @@ def tile_attndecoderrnn_kernel(tc, table, context, hid, w_e, w_c, w_h, b_ih, b_h
     ):
         offsets = held.tile([P, N // 16], U16, name="offsets")
         nc.sync.dma_start(offsets[:], offs)
+        bih = held.tile([P, GATES], F32, name="bih")
+        bhh = held.tile([P, GATES], F32, name="bhh")
+        with nc.allow_non_contiguous_dma(reason="a bias of 384 floats, one to a partition"):
+            nc.sync.dma_start(bih[:], b_ih.rearrange("(q m) o -> m (q o)", q=GATES))
+            nc.sync.dma_start(bhh[:], b_hh.rearrange("(q m) o -> m (q o)", q=GATES))
         words = held.tile([P, V], BF16, name="words")
         nc.sync.dma_start(words[:], table)
-        we = held.tile([P, GATES * P], BF16, name="we")
-        nc.scalar.dma_start(we[:], w_e)
         wc = held.tile([P, GATES * P], BF16, name="wc")
         nc.scalar.dma_start(wc[:], w_c)
         ctx = held.tile([P, N], BF16, name="ctx")
         nc.scalar.dma_start(ctx[:], context)
         wh = held.tile([P, GATES * P], BF16, name="wh")
-        nc.gpsimd.dma_start(wh[:], w_h)
+        nc.scalar.dma_start(wh[:], w_h)
         old = held.tile([P, N], BF16, name="old")
-        nc.gpsimd.dma_start(old[:], hid)
-        bih = held.tile([P, GATES], F32, name="bih")
-        bhh = held.tile([P, GATES], F32, name="bhh")
-        with nc.allow_non_contiguous_dma(reason="a bias of 384 floats, one to a partition"):
-            nc.gpsimd.dma_start(bih[:], b_ih.rearrange("(q m) o -> m (q o)", q=GATES))
-            nc.gpsimd.dma_start(bhh[:], b_hh.rearrange("(q m) o -> m (q o)", q=GATES))
+        nc.scalar.dma_start(old[:], hid)
+        we = held.tile([P, GATES * P], BF16, name="we")
+        nc.scalar.dma_start(we[:], w_e)
         bsum = held.tile([P, 2], F32, name="bsum")
         nc.vector.tensor_tensor(bsum[:], bih[:, 0:2], bhh[:, 0:2], ADD)
 

@@ -4,6 +4,7 @@ P = 128
 V = 2048
 N = 512
 GATES = 3
+HALF = N // 2
 
 FLOPS = 2 * P * P * N * 9
 BYTES = (2 * (3 * P * N + 3 * P * GATES * P)
@@ -45,35 +46,40 @@ def tile_attndecoderrnn_kernel(tc, table, context, hid, w_e, w_c, w_h, b_ih, b_h
         def gate(w, q):
             return w[:, q * P : (q + 1) * P]
 
-        picked = words[:].indirect(offsets[:])
-        acc_r = psum.tile([P, N], F32, name="acc_r")
-        acc_z = psum.tile([P, N], F32, name="acc_z")
-        acc_a = psum.tile([P, N], F32, name="acc_a")
-        acc_u = psum.tile([P, N], F32, name="acc_u")
-        nc.tensor.matmul(acc_r[:], gate(we, 0), picked, start=True, stop=False)
-        nc.tensor.matmul(acc_a[:], gate(we, 2), picked, start=True, stop=False)
-        nc.tensor.matmul(acc_z[:], gate(we, 1), picked, start=True, stop=False)
-        nc.tensor.matmul(acc_r[:], gate(wc, 0), ctx[:], start=False, stop=False)
-        nc.tensor.matmul(acc_r[:], gate(wh, 0), old[:], start=False, stop=True)
-        nc.tensor.matmul(acc_u[:], gate(wh, 2), old[:], start=True, stop=True)
-        nc.tensor.matmul(acc_a[:], gate(wc, 2), ctx[:], start=False, stop=True)
-        nc.tensor.matmul(acc_z[:], gate(wc, 1), ctx[:], start=False, stop=False)
-        nc.tensor.matmul(acc_z[:], gate(wh, 1), old[:], start=False, stop=True)
+        def half(tile, h):
+            return tile[:, h * HALF : (h + 1) * HALF]
 
-        r = held.tile([P, N], F32, name="r")
-        nc.scalar.activation(r[:], acc_r[:], SIGMOID, bias=bsum[:, 0:1])
-        ru = held.tile([P, N], F32, name="ru")
-        nc.vector.scalar_tensor_tensor(ru[:], acc_u[:], bhh[:, 2:3], r[:], ADD, MULT)
-        pre = held.tile([P, N], F32, name="pre")
-        nc.vector.tensor_tensor(pre[:], ru[:], acc_a[:], ADD)
-        n = held.tile([P, N], F32, name="n")
-        nc.scalar.activation(n[:], pre[:], TANH, bias=bih[:, 2:3])
-        z = held.tile([P, N], F32, name="z")
-        nc.scalar.activation(z[:], acc_z[:], SIGMOID, bias=bsum[:, 1:2])
-        diff = held.tile([P, N], F32, name="diff")
-        nc.vector.tensor_tensor(diff[:], old[:], n[:], SUB)
-        step = held.tile([P, N], F32, name="step")
-        nc.vector.tensor_tensor(step[:], z[:], diff[:], MULT)
-        new = held.tile([P, N], F32, name="new")
-        nc.vector.tensor_tensor(new[:], n[:], step[:], ADD)
-        nc.sync.dma_start(out, new[:])
+        acc_r = [psum.tile([P, HALF], F32, name=f"acc_r{h}") for h in range(2)]
+        acc_z = [psum.tile([P, HALF], F32, name=f"acc_z{h}") for h in range(2)]
+        acc_a = [psum.tile([P, HALF], F32, name=f"acc_a{h}") for h in range(2)]
+        acc_u = psum.tile([P, N], F32, name="acc_u")
+        for acc, q in ((acc_r, 0), (acc_a, 2), (acc_z, 1)):
+            for h in range(2):
+                nc.tensor.matmul(acc[h][:], gate(wc, q), half(ctx, h), start=True, stop=False)
+        for acc, q in ((acc_r, 0), (acc_z, 1)):
+            for h in range(2):
+                nc.tensor.matmul(acc[h][:], gate(wh, q), half(old, h), start=False, stop=False)
+        nc.tensor.matmul(acc_u[:], gate(wh, 2), old[:], start=True, stop=True)
+        for h in range(2):
+            picked = words[:].indirect(offsets[:, h * (HALF // 16) : (h + 1) * (HALF // 16)])
+            for acc, q in ((acc_r, 0), (acc_a, 2), (acc_z, 1)):
+                nc.tensor.matmul(acc[h][:], gate(we, q), picked, start=False, stop=True)
+
+        for h in range(2):
+            r = held.tile([P, HALF], F32, name=f"r{h}")
+            nc.scalar.activation(r[:], acc_r[h][:], SIGMOID, bias=bsum[:, 0:1])
+            ru = held.tile([P, HALF], F32, name=f"ru{h}")
+            nc.vector.scalar_tensor_tensor(ru[:], half(acc_u, h), bhh[:, 2:3], r[:], ADD, MULT)
+            pre = held.tile([P, HALF], F32, name=f"pre{h}")
+            nc.vector.tensor_tensor(pre[:], ru[:], acc_a[h][:], ADD)
+            n = held.tile([P, HALF], F32, name=f"n{h}")
+            nc.scalar.activation(n[:], pre[:], TANH, bias=bih[:, 2:3])
+            z = held.tile([P, HALF], F32, name=f"z{h}")
+            nc.scalar.activation(z[:], acc_z[h][:], SIGMOID, bias=bsum[:, 1:2])
+            diff = held.tile([P, HALF], F32, name=f"diff{h}")
+            nc.vector.tensor_tensor(diff[:], half(old, h), n[:], SUB)
+            step = held.tile([P, HALF], F32, name=f"step{h}")
+            nc.vector.tensor_tensor(step[:], z[:], diff[:], MULT)
+            new = held.tile([P, HALF], F32, name=f"new{h}")
+            nc.vector.tensor_tensor(new[:], n[:], step[:], ADD)
+            nc.sync.dma_start(half(out, h), new[:])

@@ -5,6 +5,7 @@ V = 2048
 N = 512
 GATES = 3
 HALF = N // 2
+WARM_UP = 6
 
 FLOPS = 2 * P * P * N * 9
 BYTES = (2 * (3 * P * N + 3 * P * GATES * P)
@@ -21,6 +22,12 @@ def tile_attndecoderrnn_kernel(tc, table, context, hid, w_e, w_c, w_h, b_ih, b_h
         tc.tile_pool(name="held", bufs=1) as held,
         tc.psum_pool(name="psum", bufs=1) as psum,
     ):
+        zeros = held.tile([P, N], BF16, name="zeros")
+        nc.vector.memset(zeros[:], 0.0)
+        idle = psum.tile([P, N], F32, name="idle")
+        for turn in range(WARM_UP):
+            nc.tensor.matmul(idle[:], zeros[:, 0:P], zeros[:], start=True, stop=True)
+
         offsets = held.tile([P, N // 16], U16, name="offsets")
         nc.sync.dma_start(offsets[:], offs)
         bih = held.tile([P, GATES], F32, name="bih")

@@ -5,7 +5,7 @@ V = 2048
 N = 512
 GATES = 3
 HALF = N // 2
-WARM_UP = 6
+WARM_UP = 16
 
 FLOPS = 2 * P * P * N * 9
 BYTES = (2 * (3 * P * N + 3 * P * GATES * P)
@@ -22,31 +22,35 @@ def tile_attndecoderrnn_kernel(tc, table, context, hid, w_e, w_c, w_h, b_ih, b_h
         tc.tile_pool(name="held", bufs=1) as held,
         tc.psum_pool(name="psum", bufs=1) as psum,
     ):
-        zeros = held.tile([P, N], BF16, name="zeros")
+        zeros = held.tile([P, P], BF16, name="zeros")
         nc.vector.memset(zeros[:], 0.0)
-        idle = psum.tile([P, N], F32, name="idle")
+        idle = psum.tile([P, P], F32, name="idle")
         for turn in range(WARM_UP):
-            nc.tensor.matmul(idle[:], zeros[:, 0:P], zeros[:], start=True, stop=True)
+            nc.tensor.matmul(idle[:], zeros[:], zeros[:], start=True, stop=True)
 
-        offsets = held.tile([P, N // 16], U16, name="offsets")
-        nc.sync.dma_start(offsets[:], offs)
-        bih = held.tile([P, GATES], F32, name="bih")
-        bhh = held.tile([P, GATES], F32, name="bhh")
-        with nc.allow_non_contiguous_dma(reason="a bias of 384 floats, one to a partition"):
-            nc.sync.dma_start(bih[:], b_ih.rearrange("(q m) o -> m (q o)", q=GATES))
-            nc.sync.dma_start(bhh[:], b_hh.rearrange("(q m) o -> m (q o)", q=GATES))
+        wc = held.tile([P, GATES * P], BF16, name="wc")
+        nc.sync.dma_start(wc[:], w_c)
+        ctx = held.tile([P, N], BF16, name="ctx")
+        nc.sync.dma_start(ctx[:], context)
         words = held.tile([P, V], BF16, name="words")
         nc.sync.dma_start(words[:], table)
-        wc = held.tile([P, GATES * P], BF16, name="wc")
-        nc.scalar.dma_start(wc[:], w_c)
-        ctx = held.tile([P, N], BF16, name="ctx")
-        nc.scalar.dma_start(ctx[:], context)
+        offsets = held.tile([P, N // 16], U16, name="offsets")
+        nc.sync.dma_start(offsets[:], offs)
         wh = held.tile([P, GATES * P], BF16, name="wh")
         nc.scalar.dma_start(wh[:], w_h)
         old = held.tile([P, N], BF16, name="old")
         nc.scalar.dma_start(old[:], hid)
         we = held.tile([P, GATES * P], BF16, name="we")
         nc.scalar.dma_start(we[:], w_e)
+        bih = held.tile([P, GATES], F32, name="bih")
+        bhh = held.tile([P, GATES], F32, name="bhh")
+        with nc.allow_non_contiguous_dma(reason="a bias of 384 floats, one to a partition"):
+            nc.scalar.dma_start(bih[:], b_ih.rearrange("(q m) o -> m (q o)", q=GATES))
+            nc.scalar.dma_start(bhh[:], b_hh.rearrange("(q m) o -> m (q o)", q=GATES))
+
+        early = held.tile([P, 1], F32, name="early")
+        nc.scalar.activation(early[:], zeros[:, 0:1], SIGMOID)
+
         bsum = held.tile([P, 2], F32, name="bsum")
         nc.vector.tensor_tensor(bsum[:], bih[:, 0:2], bhh[:, 0:2], ADD)
 
@@ -67,10 +71,10 @@ def tile_attndecoderrnn_kernel(tc, table, context, hid, w_e, w_c, w_h, b_ih, b_h
             for h in range(2):
                 nc.tensor.matmul(acc[h][:], gate(wh, q), half(old, h), start=False, stop=False)
         nc.tensor.matmul(acc_u[:], gate(wh, 2), old[:], start=True, stop=True)
-        for h in range(2):
-            picked = words[:].indirect(offsets[:, h * (HALF // 16) : (h + 1) * (HALF // 16)])
-            for acc, q in ((acc_r, 0), (acc_a, 2), (acc_z, 1)):
-                nc.tensor.matmul(acc[h][:], gate(we, q), picked, start=False, stop=True)
+        picked = [words[:].indirect(offsets[:, h * (HALF // 16) : (h + 1) * (HALF // 16)]) for h in range(2)]
+        for acc, q in ((acc_r, 0), (acc_a, 2), (acc_z, 1)):
+            for h in range(2):
+                nc.tensor.matmul(acc[h][:], gate(we, q), picked[h], start=False, stop=True)
 
         for h in range(2):
             r = held.tile([P, HALF], F32, name=f"r{h}")
@@ -83,10 +87,10 @@ def tile_attndecoderrnn_kernel(tc, table, context, hid, w_e, w_c, w_h, b_ih, b_h
             nc.scalar.activation(n[:], pre[:], TANH, bias=bih[:, 2:3])
             z = held.tile([P, HALF], F32, name=f"z{h}")
             nc.scalar.activation(z[:], acc_z[h][:], SIGMOID, bias=bsum[:, 1:2])
-            diff = held.tile([P, HALF], F32, name=f"diff{h}")
-            nc.vector.tensor_tensor(diff[:], half(old, h), n[:], SUB)
-            step = held.tile([P, HALF], F32, name=f"step{h}")
-            nc.vector.tensor_tensor(step[:], z[:], diff[:], MULT)
+            carry = held.tile([P, HALF], F32, name=f"carry{h}")
+            nc.vector.tensor_tensor(carry[:], z[:], half(old, h), MULT)
+            gone = held.tile([P, HALF], F32, name=f"gone{h}")
+            nc.vector.scalar_tensor_tensor(gone[:], z[:], 1.0, n[:], SUB, MULT)
             new = held.tile([P, HALF], F32, name=f"new{h}")
-            nc.vector.tensor_tensor(new[:], n[:], step[:], ADD)
+            nc.vector.tensor_tensor(new[:], carry[:], gone[:], SUB)
             nc.sync.dma_start(half(out, h), new[:])

@@ -72,7 +72,7 @@ def tile_attndecoderrnn_kernel(tc, table, context, hid, w_e, w_c, w_h, b_ih, b_h
                 nc.tensor.matmul(acc[h][:], gate(wh, q), half(old, h), start=False, stop=False)
         nc.tensor.matmul(acc_u[:], gate(wh, 2), old[:], start=True, stop=True)
         picked = [words[:].indirect(offsets[:, h * (HALF // 16) : (h + 1) * (HALF // 16)]) for h in range(2)]
-        for acc, q in ((acc_r, 0), (acc_a, 2), (acc_z, 1)):
+        for acc, q in ((acc_r, 0), (acc_z, 1), (acc_a, 2)):
             for h in range(2):
                 nc.tensor.matmul(acc[h][:], gate(we, q), picked[h], start=False, stop=True)
 
@@ -88,7 +88,7 @@ def tile_attndecoderrnn_kernel(tc, table, context, hid, w_e, w_c, w_h, b_ih, b_h
             z = held.tile([P, HALF], F32, name=f"z{h}")
             nc.scalar.activation(z[:], acc_z[h][:], SIGMOID, bias=bsum[:, 1:2])
             carry = held.tile([P, HALF], F32, name=f"carry{h}")
-            nc.vector.tensor_tensor(carry[:], z[:], half(old, h), MULT)
+            nc.gpsimd.tensor_tensor(carry[:], z[:], half(old, h), MULT)
             gone = held.tile([P, HALF], F32, name=f"gone{h}")
             nc.vector.scalar_tensor_tensor(gone[:], z[:], 1.0, n[:], SUB, MULT)
             new = held.tile([P, HALF], F32, name=f"new{h}")

@@ -6,6 +6,7 @@ N = 512
 GATES = 3
 HALF = N // 2
 WARM_UP = 16
+BLOCK = 32
 
 FLOPS = 2 * P * P * N * 9
 BYTES = (2 * (3 * P * N + 3 * P * GATES * P)
@@ -22,6 +23,18 @@ def tile_attndecoderrnn_kernel(tc, table, context, hid, w_e, w_c, w_h, b_ih, b_h
         tc.tile_pool(name="held", bufs=1) as held,
         tc.psum_pool(name="psum", bufs=1) as psum,
     ):
+        lying = held.tile([P, 2 * P], F32, name="lying", align_bytes=64)
+        nc.vector.memset(lying[:], 0.0)
+        for k, bias in enumerate((b_ih, b_hh)):
+            nc.scalar.dma_start(
+                lying[0:P:BLOCK, k * GATES * BLOCK : (k + 1) * GATES * BLOCK].rearrange("g (q i) -> g q i", q=GATES),
+                bias.rearrange("(q g i) o -> g q (i o)", q=GATES, g=P // BLOCK),
+            )
+        standing = held.tile([P, 2 * P], F32, name="standing", align_bytes=64)
+        nc.vector.transpose(standing[:], lying[:])
+        bih = standing[:, 0 : GATES * BLOCK : BLOCK]
+        bhh = standing[:, GATES * BLOCK : 2 * GATES * BLOCK : BLOCK]
+
         zeros = held.tile([P, P], BF16, name="zeros")
         nc.vector.memset(zeros[:], 0.0)
         idle = psum.tile([P, P], F32, name="idle")
@@ -42,11 +55,6 @@ def tile_attndecoderrnn_kernel(tc, table, context, hid, w_e, w_c, w_h, b_ih, b_h
         nc.scalar.dma_start(old[:], hid)
         we = held.tile([P, GATES * P], BF16, name="we")
         nc.scalar.dma_start(we[:], w_e)
-        bih = held.tile([P, GATES], F32, name="bih")
-        bhh = held.tile([P, GATES], F32, name="bhh")
-        with nc.allow_non_contiguous_dma(reason="a bias of 384 floats, one to a partition"):
-            nc.scalar.dma_start(bih[:], b_ih.rearrange("(q m) o -> m (q o)", q=GATES))
-            nc.scalar.dma_start(bhh[:], b_hh.rearrange("(q m) o -> m (q o)", q=GATES))
 
         early = held.tile([P, 1], F32, name="early")
         nc.scalar.activation(early[:], zeros[:, 0:1], SIGMOID)

@@ -23,6 +23,12 @@ def tile_attndecoderrnn_kernel(tc, table, context, hid, w_e, w_c, w_h, b_ih, b_h
         tc.tile_pool(name="held", bufs=1) as held,
         tc.psum_pool(name="psum", bufs=1) as psum,
     ):
+        zeros = held.tile([P, P], BF16, name="zeros")
+        nc.vector.memset(zeros[:], 0.0)
+        idle = psum.tile([P, P], F32, name="idle")
+        for turn in range(WARM_UP):
+            nc.tensor.matmul(idle[:], zeros[:], zeros[:], start=True, stop=True)
+
         lying = held.tile([P, 2 * P], F32, name="lying", align_bytes=64)
         nc.vector.memset(lying[:], 0.0)
         for k, bias in enumerate((b_ih, b_hh)):
@@ -34,12 +40,6 @@ def tile_attndecoderrnn_kernel(tc, table, context, hid, w_e, w_c, w_h, b_ih, b_h
         nc.vector.transpose(standing[:], lying[:])
         bih = standing[:, 0 : GATES * BLOCK : BLOCK]
         bhh = standing[:, GATES * BLOCK : 2 * GATES * BLOCK : BLOCK]
-
-        zeros = held.tile([P, P], BF16, name="zeros")
-        nc.vector.memset(zeros[:], 0.0)
-        idle = psum.tile([P, P], F32, name="idle")
-        for turn in range(WARM_UP):
-            nc.tensor.matmul(idle[:], zeros[:], zeros[:], start=True, stop=True)
 
         wc = held.tile([P, GATES * P], BF16, name="wc")
         nc.sync.dma_start(wc[:], w_c)

@@ -41,14 +41,14 @@ def tile_attndecoderrnn_kernel(tc, table, context, hid, w_e, w_c, w_h, b_ih, b_h
         bih = standing[:, 0 : GATES * BLOCK : BLOCK]
         bhh = standing[:, GATES * BLOCK : 2 * GATES * BLOCK : BLOCK]
 
+        offsets = held.tile([P, N // 16], U16, name="offsets")
+        nc.sync.dma_start(offsets[:], offs)
         wc = held.tile([P, GATES * P], BF16, name="wc")
         nc.sync.dma_start(wc[:], w_c)
         ctx = held.tile([P, N], BF16, name="ctx")
         nc.sync.dma_start(ctx[:], context)
         words = held.tile([P, V], BF16, name="words")
         nc.sync.dma_start(words[:], table)
-        offsets = held.tile([P, N // 16], U16, name="offsets")
-        nc.sync.dma_start(offsets[:], offs)
         wh = held.tile([P, GATES * P], BF16, name="wh")
         nc.scalar.dma_start(wh[:], w_h)
         old = held.tile([P, N], BF16, name="old")

@@ -87,7 +87,7 @@ def tile_attndecoderrnn_kernel(tc, table, context, hid, w_e, w_c, w_h, b_ih, b_h
         for h in range(2):
             r = held.tile([P, HALF], F32, name=f"r{h}")
             nc.scalar.activation(r[:], acc_r[h][:], SIGMOID, bias=bsum[:, 0:1])
-            ru = held.tile([P, HALF], F32, name=f"ru{h}")
+            ru = held.tile([P, HALF], F32, name=f"ru{h}", tag=f"ru{h}")
             nc.vector.scalar_tensor_tensor(ru[:], half(acc_u, h), bhh[:, 2:3], r[:], ADD, MULT)
             pre = held.tile([P, HALF], F32, name=f"pre{h}")
             nc.vector.tensor_tensor(pre[:], ru[:], acc_a[h][:], ADD)
@@ -95,8 +95,9 @@ def tile_attndecoderrnn_kernel(tc, table, context, hid, w_e, w_c, w_h, b_ih, b_h
             nc.scalar.activation(n[:], pre[:], TANH, bias=bih[:, 2:3])
             z = held.tile([P, HALF], F32, name=f"z{h}")
             nc.scalar.activation(z[:], acc_z[h][:], SIGMOID, bias=bsum[:, 1:2])
-            carry = held.tile([P, HALF], F32, name=f"carry{h}")
-            nc.gpsimd.tensor_tensor(carry[:], z[:], half(old, h), MULT)
+            engine = nc.gpsimd if h == 0 else nc.vector
+            carry = held.tile([P, HALF], F32, name=f"carry{h}", tag="carry0" if h == 0 else "ru0")
+            engine.tensor_tensor(carry[:], z[:], half(old, h), MULT)
             gone = held.tile([P, HALF], F32, name=f"gone{h}")
             nc.vector.scalar_tensor_tensor(gone[:], z[:], 1.0, n[:], SUB, MULT)
             new = held.tile([P, HALF], F32, name=f"new{h}")

@@ -80,26 +80,34 @@ def tile_attndecoderrnn_kernel(tc, table, context, hid, w_e, w_c, w_h, b_ih, b_h
                 nc.tensor.matmul(acc[h][:], gate(wh, q), half(old, h), start=False, stop=False)
         nc.tensor.matmul(acc_u[:], gate(wh, 2), old[:], start=True, stop=True)
         picked = [words[:].indirect(offsets[:, h * (HALF // 16) : (h + 1) * (HALF // 16)]) for h in range(2)]
-        for acc, q in ((acc_r, 0), (acc_z, 1), (acc_a, 2)):
-            for h in range(2):
+        for acc, q, order in ((acc_r, 0, (0, 1)), (acc_z, 1, (1, 0)), (acc_a, 2, (0, 1))):
+            for h in order:
                 nc.tensor.matmul(acc[h][:], gate(we, q), picked[h], start=False, stop=True)
 
-        for h in range(2):
-            r = held.tile([P, HALF], F32, name=f"r{h}")
-            nc.scalar.activation(r[:], acc_r[h][:], SIGMOID, bias=bsum[:, 0:1])
-            ru = held.tile([P, HALF], F32, name=f"ru{h}", tag=f"ru{h}")
-            nc.vector.scalar_tensor_tensor(ru[:], half(acc_u, h), bhh[:, 2:3], r[:], ADD, MULT)
-            pre = held.tile([P, HALF], F32, name=f"pre{h}")
-            nc.vector.tensor_tensor(pre[:], ru[:], acc_a[h][:], ADD)
-            n = held.tile([P, HALF], F32, name=f"n{h}")
-            nc.scalar.activation(n[:], pre[:], TANH, bias=bih[:, 2:3])
-            z = held.tile([P, HALF], F32, name=f"z{h}")
-            nc.scalar.activation(z[:], acc_z[h][:], SIGMOID, bias=bsum[:, 1:2])
-            engine = nc.gpsimd if h == 0 else nc.vector
-            carry = held.tile([P, HALF], F32, name=f"carry{h}", tag="carry0" if h == 0 else "ru0")
-            engine.tensor_tensor(carry[:], z[:], half(old, h), MULT)
-            gone = held.tile([P, HALF], F32, name=f"gone{h}")
-            nc.vector.scalar_tensor_tensor(gone[:], z[:], 1.0, n[:], SUB, MULT)
-            new = held.tile([P, HALF], F32, name=f"new{h}")
-            nc.vector.tensor_tensor(new[:], carry[:], gone[:], SUB)
-            nc.sync.dma_start(half(out, h), new[:])
+        halves = range(2)
+        r = [held.tile([P, HALF], F32, name=f"r{h}") for h in halves]
+        ru = [held.tile([P, HALF], F32, name=f"ru{h}", tag=f"ru{h}") for h in halves]
+        pre = [held.tile([P, HALF], F32, name=f"pre{h}") for h in halves]
+        n = [held.tile([P, HALF], F32, name=f"n{h}") for h in halves]
+        z = [held.tile([P, HALF], F32, name=f"z{h}") for h in halves]
+        gone = [held.tile([P, HALF], F32, name=f"gone{h}") for h in halves]
+        new = [held.tile([P, HALF], F32, name=f"new{h}") for h in halves]
+        for h in halves:
+            nc.scalar.activation(r[h][:], acc_r[h][:], SIGMOID, bias=bsum[:, 0:1])
+        for h in (1, 0):
+            nc.scalar.activation(z[h][:], acc_z[h][:], SIGMOID, bias=bsum[:, 1:2])
+        for h in halves:
+            nc.vector.scalar_tensor_tensor(ru[h][:], half(acc_u, h), bhh[:, 2:3], r[h][:], ADD, MULT)
+        for h in halves:
+            nc.vector.tensor_tensor(pre[h][:], ru[h][:], acc_a[h][:], ADD)
+        for h in halves:
+            nc.scalar.activation(n[h][:], pre[h][:], TANH, bias=bih[:, 2:3])
+        carry1 = held.tile([P, HALF], F32, name="carry1")
+        nc.gpsimd.tensor_tensor(carry1[:], z[1][:], half(old, 1), MULT)
+        carry0 = held.tile([P, HALF], F32, name="carry0", tag="ru0")
+        nc.vector.tensor_tensor(carry0[:], z[0][:], half(old, 0), MULT)
+        for h in halves:
+            nc.vector.scalar_tensor_tensor(gone[h][:], z[h][:], 1.0, n[h][:], SUB, MULT)
+        for h, carry in enumerate((carry0, carry1)):
+            nc.vector.tensor_tensor(new[h][:], carry[:], gone[h][:], SUB)
+            nc.sync.dma_start(half(out, h), new[h][:])

@@ -5,7 +5,8 @@ V = 2048
 N = 512
 GATES = 3
 HALF = N // 2
-WARM_UP = 16
+WARM_UP = 4
+STRIP = 32
 BLOCK = 32
 
 FLOPS = 2 * P * P * N * 9
@@ -23,23 +24,11 @@ def tile_attndecoderrnn_kernel(tc, table, context, hid, w_e, w_c, w_h, b_ih, b_h
         tc.tile_pool(name="held", bufs=1) as held,
         tc.psum_pool(name="psum", bufs=1) as psum,
     ):
-        zeros = held.tile([P, P], BF16, name="zeros")
+        zeros = held.tile([P, STRIP], BF16, name="zeros")
         nc.vector.memset(zeros[:], 0.0)
-        idle = psum.tile([P, P], F32, name="idle")
+        idle = psum.tile([STRIP, N], F32, name="idle")
         for turn in range(WARM_UP):
-            nc.tensor.matmul(idle[:], zeros[:], zeros[:], start=True, stop=True)
-
-        lying = held.tile([P, 2 * P], F32, name="lying", align_bytes=64)
-        nc.vector.memset(lying[:], 0.0)
-        for k, bias in enumerate((b_ih, b_hh)):
-            nc.scalar.dma_start(
-                lying[0:P:BLOCK, k * GATES * BLOCK : (k + 1) * GATES * BLOCK].rearrange("g (q i) -> g q i", q=GATES),
-                bias.rearrange("(q g i) o -> g q (i o)", q=GATES, g=P // BLOCK),
-            )
-        standing = held.tile([P, 2 * P], F32, name="standing", align_bytes=64)
-        nc.vector.transpose(standing[:], lying[:])
-        bih = standing[:, 0 : GATES * BLOCK : BLOCK]
-        bhh = standing[:, GATES * BLOCK : 2 * GATES * BLOCK : BLOCK]
+            nc.tensor.matmul(idle[:], zeros[:], zeros[:, 0:1].to_broadcast([P, N]), start=True, stop=True)
 
         offsets = held.tile([P, N // 16], U16, name="offsets")
         nc.sync.dma_start(offsets[:], offs)
@@ -53,6 +42,19 @@ def tile_attndecoderrnn_kernel(tc, table, context, hid, w_e, w_c, w_h, b_ih, b_h
         nc.scalar.dma_start(wh[:], w_h)
         old = held.tile([P, N], BF16, name="old")
         nc.scalar.dma_start(old[:], hid)
+
+        lying = held.tile([P, P], F32, name="lying", align_bytes=64)
+        nc.vector.memset(lying[:], 0.0)
+        for k, bias in enumerate((b_ih, b_hh)):
+            nc.scalar.dma_start(
+                lying[k:P:BLOCK, 0 : GATES * BLOCK].rearrange("g (q i) -> g q i", q=GATES),
+                bias.rearrange("(q g i) o -> g q (i o)", q=GATES, g=P // BLOCK),
+            )
+        standing = held.tile([P, P], F32, name="standing", align_bytes=64)
+        nc.vector.transpose(standing[:], lying[:])
+        bih = standing[:, 0 : GATES * BLOCK : BLOCK]
+        bhh = standing[:, 1 : GATES * BLOCK : BLOCK]
+
         we = held.tile([P, GATES * P], BF16, name="we")
         nc.scalar.dma_start(we[:], w_e)
 
@@ -72,17 +74,17 @@ def tile_attndecoderrnn_kernel(tc, table, context, hid, w_e, w_c, w_h, b_ih, b_h
         acc_z = [psum.tile([P, HALF], F32, name=f"acc_z{h}") for h in range(2)]
         acc_a = [psum.tile([P, HALF], F32, name=f"acc_a{h}") for h in range(2)]
         acc_u = psum.tile([P, N], F32, name="acc_u")
-        for acc, q in ((acc_r, 0), (acc_a, 2), (acc_z, 1)):
-            for h in range(2):
-                nc.tensor.matmul(acc[h][:], gate(wc, q), half(ctx, h), start=True, stop=False)
+        for acc, q, h in ((acc_r, 0, 0), (acc_r, 0, 1), (acc_a, 2, 0), (acc_z, 1, 0), (acc_z, 1, 1)):
+            nc.tensor.matmul(acc[h][:], gate(wc, q), half(ctx, h), start=True, stop=False)
         for acc, q in ((acc_r, 0), (acc_z, 1)):
             for h in range(2):
                 nc.tensor.matmul(acc[h][:], gate(wh, q), half(old, h), start=False, stop=False)
         nc.tensor.matmul(acc_u[:], gate(wh, 2), old[:], start=True, stop=True)
         picked = [words[:].indirect(offsets[:, h * (HALF // 16) : (h + 1) * (HALF // 16)]) for h in range(2)]
-        for acc, q, order in ((acc_r, 0, (0, 1)), (acc_z, 1, (1, 0)), (acc_a, 2, (0, 1))):
-            for h in order:
-                nc.tensor.matmul(acc[h][:], gate(we, q), picked[h], start=False, stop=True)
+        for acc, q, h in ((acc_r, 0, 0), (acc_r, 0, 1), (acc_z, 1, 1), (acc_z, 1, 0), (acc_a, 2, 0)):
+            nc.tensor.matmul(acc[h][:], gate(we, q), picked[h], start=False, stop=True)
+        nc.tensor.matmul(acc_a[1][:], gate(we, 2), picked[1], start=True, stop=False)
+        nc.tensor.matmul(acc_a[1][:], gate(wc, 2), half(ctx, 1), start=False, stop=True)
 
         halves = range(2)
         r = [held.tile([P, HALF], F32, name=f"r{h}") for h in halves]

import concourse.mybir as mybir

P = 128
V = 2048
N = 512
GATES = 3
HALF = N // 2
WARM_UP = 4
STRIP = 32
BLOCK = 32

FLOPS = 2 * P * P * N * 9
BYTES = (2 * (3 * P * N + 3 * P * GATES * P)
         + 4 * 2 * GATES * P + 2 * N + 4 * P * N)

BF16, F32, U16 = mybir.dt.bfloat16, mybir.dt.float32, mybir.dt.uint16
ADD, SUB, MULT = mybir.AluOpType.add, mybir.AluOpType.subtract, mybir.AluOpType.mult
SIGMOID, TANH = mybir.ActivationFunctionType.Sigmoid, mybir.ActivationFunctionType.Tanh


def tile_attndecoderrnn_kernel(tc, table, context, hid, w_e, w_c, w_h, b_ih, b_hh, offs, out):
    nc = tc.nc
    with (
        tc.tile_pool(name="held", bufs=1) as held,
        tc.psum_pool(name="psum", bufs=1) as psum,
    ):
        zeros = held.tile([P, STRIP], BF16, name="zeros")
        nc.vector.memset(zeros[:], 0.0)
        idle = psum.tile([STRIP, N], F32, name="idle")
        for turn in range(WARM_UP):
            nc.tensor.matmul(idle[:], zeros[:], zeros[:, 0:1].to_broadcast([P, N]), start=True, stop=True)

        offsets = held.tile([P, N // 16], U16, name="offsets")
        nc.sync.dma_start(offsets[:], offs)
        wc = held.tile([P, GATES * P], BF16, name="wc")
        nc.sync.dma_start(wc[:], w_c)
        ctx = held.tile([P, N], BF16, name="ctx")
        nc.sync.dma_start(ctx[:], context)
        words = held.tile([P, V], BF16, name="words")
        nc.sync.dma_start(words[:], table)
        wh = held.tile([P, GATES * P], BF16, name="wh")
        nc.scalar.dma_start(wh[:], w_h)
        old = held.tile([P, N], BF16, name="old")
        nc.scalar.dma_start(old[:], hid)

        lying = held.tile([P, P], F32, name="lying", align_bytes=64)
        nc.vector.memset(lying[:], 0.0)
        for k, bias in enumerate((b_ih, b_hh)):
            nc.scalar.dma_start(
                lying[k:P:BLOCK, 0 : GATES * BLOCK].rearrange("g (q i) -> g q i", q=GATES),
                bias.rearrange("(q g i) o -> g q (i o)", q=GATES, g=P // BLOCK),
            )
        standing = held.tile([P, P], F32, name="standing", align_bytes=64)
        nc.vector.transpose(standing[:], lying[:])
        bih = standing[:, 0 : GATES * BLOCK : BLOCK]
        bhh = standing[:, 1 : GATES * BLOCK : BLOCK]

        we = held.tile([P, GATES * P], BF16, name="we")
        nc.scalar.dma_start(we[:], w_e)

        early = held.tile([P, 1], F32, name="early")
        nc.scalar.activation(early[:], zeros[:, 0:1], SIGMOID)

        bsum = held.tile([P, 2], F32, name="bsum")
        nc.vector.tensor_tensor(bsum[:], bih[:, 0:2], bhh[:, 0:2], ADD)

        def gate(w, q):
            return w[:, q * P : (q + 1) * P]

        def half(tile, h):
            return tile[:, h * HALF : (h + 1) * HALF]

        acc_r = [psum.tile([P, HALF], F32, name=f"acc_r{h}") for h in range(2)]
        acc_z = [psum.tile([P, HALF], F32, name=f"acc_z{h}") for h in range(2)]
        acc_a = [psum.tile([P, HALF], F32, name=f"acc_a{h}") for h in range(2)]
        acc_u = psum.tile([P, N], F32, name="acc_u")
        for acc, q, h in ((acc_r, 0, 0), (acc_r, 0, 1), (acc_a, 2, 0), (acc_z, 1, 0), (acc_z, 1, 1)):
            nc.tensor.matmul(acc[h][:], gate(wc, q), half(ctx, h), start=True, stop=False)
        for acc, q in ((acc_r, 0), (acc_z, 1)):
            for h in range(2):
                nc.tensor.matmul(acc[h][:], gate(wh, q), half(old, h), start=False, stop=False)
        nc.tensor.matmul(acc_u[:], gate(wh, 2), old[:], start=True, stop=True)
        picked = [words[:].indirect(offsets[:, h * (HALF // 16) : (h + 1) * (HALF // 16)]) for h in range(2)]
        for acc, q, h in ((acc_r, 0, 0), (acc_r, 0, 1), (acc_z, 1, 1), (acc_z, 1, 0), (acc_a, 2, 0)):
            nc.tensor.matmul(acc[h][:], gate(we, q), picked[h], start=False, stop=True)
        nc.tensor.matmul(acc_a[1][:], gate(we, 2), picked[1], start=True, stop=False)
        nc.tensor.matmul(acc_a[1][:], gate(wc, 2), half(ctx, 1), start=False, stop=True)

        halves = range(2)
        r = [held.tile([P, HALF], F32, name=f"r{h}") for h in halves]
        ru = [held.tile([P, HALF], F32, name=f"ru{h}", tag=f"ru{h}") for h in halves]
        pre = [held.tile([P, HALF], F32, name=f"pre{h}") for h in halves]
        n = [held.tile([P, HALF], F32, name=f"n{h}") for h in halves]
        z = [held.tile([P, HALF], F32, name=f"z{h}") for h in halves]
        gone = [held.tile([P, HALF], F32, name=f"gone{h}") for h in halves]
        new = [held.tile([P, HALF], F32, name=f"new{h}") for h in halves]
        for h in halves:
            nc.scalar.activation(r[h][:], acc_r[h][:], SIGMOID, bias=bsum[:, 0:1])
        for h in (1, 0):
            nc.scalar.activation(z[h][:], acc_z[h][:], SIGMOID, bias=bsum[:, 1:2])
        for h in halves:
            nc.vector.scalar_tensor_tensor(ru[h][:], half(acc_u, h), bhh[:, 2:3], r[h][:], ADD, MULT)
        for h in halves:
            nc.vector.tensor_tensor(pre[h][:], ru[h][:], acc_a[h][:], ADD)
        for h in halves:
            nc.scalar.activation(n[h][:], pre[h][:], TANH, bias=bih[:, 2:3])
        carry1 = held.tile([P, HALF], F32, name="carry1")
        nc.gpsimd.tensor_tensor(carry1[:], z[1][:], half(old, 1), MULT)
        carry0 = held.tile([P, HALF], F32, name="carry0", tag="ru0")
        nc.vector.tensor_tensor(carry0[:], z[0][:], half(old, 0), MULT)
        for h in halves:
            nc.vector.scalar_tensor_tensor(gone[h][:], z[h][:], 1.0, n[h][:], SUB, MULT)
        for h, carry in enumerate((carry0, carry1)):
            nc.vector.tensor_tensor(new[h][:], carry[:], gone[h][:], SUB)
            nc.sync.dma_start(half(out, h), new[h][:])
